import numpy as np
import ml_dtypes


def mxq(x, axis, fmt="e4m3"):
    dtype, down = {"e4m3": (ml_dtypes.float8_e4m3fn, 7), "e5m2": (ml_dtypes.float8_e5m2, 14)}[fmt]
    v = np.moveaxis(np.asarray(x, np.float32).astype(ml_dtypes.bfloat16).astype(np.float64), axis, -1)
    blocks = v.reshape(v.shape[:-1] + (-1, 32))
    amax = np.abs(blocks).max(-1, keepdims=True)
    byte = np.maximum(np.where(amax > 0, np.frexp(amax)[1] - 1 + 127, 0) - down, 1)
    scale = np.exp2(byte - 127.0)
    codes = (blocks / scale).astype(np.float32).astype(dtype).astype(np.float64)
    return np.moveaxis((codes * scale).reshape(v.shape), -1, axis)


WIDE = False


def mx_kscale(k):
    if not WIDE:
        return np.ones(k)
    levels = np.array([10, -10, 5, -5, 0])
    a = np.random.permutation(np.resize(levels, k // 512 * 4)).reshape(k // 512, 4)
    idx = np.arange(k)
    return np.exp2(a[idx // 512, idx % 128 // 32])


BF16 = ml_dtypes.bfloat16


def bf(x):
    return np.asarray(x, np.float32).astype(BF16)


def f64(x):
    return np.asarray(x).astype(np.float64)


E2M1 = np.array([0.0, 0.5, 1.0, 1.5, 2.0, 3.0, 4.0, 6.0, -0.0, -0.5, -1.0, -1.5, -2.0, -3.0, -4.0, -6.0])


def pack_weight(w, fmt):
    k, n = w.shape
    w = f64(bf(w)).reshape(k // 32, 32, n)
    amax = np.abs(w).max(1)
    if fmt == "e4m3":
        byte = np.frexp(amax)[1] - 1 + 127 - 7
    else:
        mant, ex = np.frexp(amax / 6.0)
        byte = np.where(mant > 0.5, ex, ex - 1) + 127
    byte = np.clip(np.where(amax > 0, byte, 1), 1, 254)
    scaled = (w * np.exp2(127.0 - byte)[:, None, :]).reshape(k, n).astype(np.float32)
    by_word = np.ascontiguousarray(scaled.reshape(k // 512, 128, 4, n).transpose(0, 1, 3, 2))
    if fmt == "e4m3":
        words = by_word.astype(ml_dtypes.float8_e4m3fn).view(np.uint8)
    else:
        c = by_word.astype(ml_dtypes.float4_e2m1fn).view(np.uint8) & 0xF
        words = c[..., 0::2] | (c[..., 1::2] << 4)
    return np.ascontiguousarray(words), np.ascontiguousarray(byte.astype(np.uint8).reshape(k // 512, 16, n))


def unpack_weight(words, scales, fmt):
    g, p, n, _ = words.shape
    if fmt == "e4m3":
        vals = np.ascontiguousarray(words).view(ml_dtypes.float8_e4m3fn).astype(np.float64)
    else:
        nib = np.empty((g, p, n, 4), np.uint8)
        nib[..., 0::2] = words & 0xF
        nib[..., 1::2] = words >> 4
        vals = E2M1[nib]
    vals = vals * np.repeat(np.exp2(scales.astype(np.float64) - 127.0), 8, axis=1)[..., None]
    return vals.transpose(0, 1, 3, 2).reshape(g * 512, n)


N, K, H, A = 128, 2, 1024, 3
D = K * H
T = A * H
FMT = "e4m3"


def sigmoid(v):
    return 1.0 / (1.0 + np.exp(-v))


def setup_inputs():
    s = mx_kscale(D)
    h_mail = np.random.standard_normal((N, K, H)) * s.reshape(K, H)
    c_mail = np.random.standard_normal((N, K, H))
    U_f_w = np.random.standard_normal((T, T)) / np.sqrt(D)
    U_f_w[:D] = U_f_w[:D] / s[:, None]
    U_f_b = np.random.standard_normal(T) * 0.5
    U_iou_w = np.random.standard_normal((3 * H, T)) / np.sqrt(D)
    U_iou_w[:, :D] = U_iou_w[:, :D] / s
    b_iou = np.random.standard_normal((1, 3 * H)) * 0.3
    U_f_w_words, U_f_w_scales = pack_weight(U_f_w, FMT)
    U_iou_w_words, U_iou_w_scales = pack_weight(np.ascontiguousarray(U_iou_w.T), FMT)
    return {"h_mail": bf(h_mail), "c_mail": bf(c_mail), "U_f_w_words": U_f_w_words, "U_f_w_scales": U_f_w_scales, "U_f_b": bf(U_f_b), "U_iou_w_words": U_iou_w_words, "U_iou_w_scales": U_iou_w_scales, "b_iou": bf(b_iou)}


def reference(h_mail, c_mail, U_f_w_words, U_f_w_scales, U_f_b, U_iou_w_words, U_iou_w_scales, b_iou):
    n, k, h = h_mail.shape
    d = k * h
    hq = mxq(f64(h_mail).reshape(n, d), 1, "e4m3")
    f = sigmoid((hq @ unpack_weight(U_f_w_words, U_f_w_scales, FMT)[:d, :d]) + f64(U_f_b)[:d])
    c_red = np.sum(f.reshape(n, k, h) * f64(c_mail), axis=1)
    iou = (hq @ unpack_weight(U_iou_w_words, U_iou_w_scales, FMT)[:d, :]) + f64(b_iou)
    i, o, u = np.split(iou, 3, axis=1)
    c = sigmoid(i) * np.tanh(u) + c_red
    h_out = sigmoid(o) * np.tanh(c)
    return h_out, c

@@ -1,0 +1,206 @@
+from contextlib import ExitStack
+
+import concourse.mybir as mybir
+from concourse.masks import make_identity
+
+F32 = mybir.dt.float32
+BF16 = mybir.dt.bfloat16
+I32 = mybir.dt.int32
+U8 = mybir.dt.uint8
+FP8X4 = mybir.dt.float8_e4m3fn_x4
+ACT = mybir.ActivationFunctionType
+ALU = mybir.AluOpType
+
+P = 128
+H = 1024
+D = 2 * H
+G = 4
+FLOPS = 2 * P * D * (D + 3 * H)
+BYTES = 2 * (P * D * 2) + G * P * (D + 3 * H) * 4 + G * 16 * (D + 3 * H) + (D + 3 * H) * 2 + 2 * P * H * 4
+
+SCALES_IOU = "mid"
+SCALES_F = "sync"
+
+
+def tile_treelstmcell_w_kernel(
+    tc, h_mail, c_mail, U_f_w_words, U_f_w_scales, U_f_b, U_iou_w_words, U_iou_w_scales, b_iou, out_0, out_1
+):
+    nc = tc.nc
+    with ExitStack() as ctx:
+        ctx.enter_context(tc.manual_schedule())
+        sb = ctx.enter_context(tc.tile_pool(name="sb", bufs=1))
+        ps = ctx.enter_context(tc.psum_pool(name="ps", bufs=1))
+
+        def bank(b, shape, dtype, name):
+            return ps.tile(shape, dtype, name=name, tag="bank%d" % b)
+
+        h_sb = sb.tile([P, D], BF16, name="h_sb")
+        c_sb = sb.tile([P, D], BF16, name="c_sb")
+        planes_f = sb.tile([P, D], U8, name="planes_f", align_bytes=64)
+        planes_iou = sb.tile([P, 3 * H], U8, name="planes_iou", align_bytes=64)
+        wf = [sb.tile([P, D], I32, name="wf%d" % g, align_bytes=64) for g in range(G)]
+        wu = [sb.tile([P, H], I32, name="wu%d" % g, align_bytes=64) for g in range(G)]
+        wi = [sb.tile([P, H], I32, name="wi%d" % g, align_bytes=64) for g in range(G - 1)]
+        wi3 = [sb.tile([P, 512], I32, name="wi3_%d" % s, align_bytes=64) for s in range(2)]
+        wo_h0 = sb.tile([P, G, 512], I32, name="wo_h0", align_bytes=64)
+        wo_h1 = sb.tile([P, G - 1, 512], I32, name="wo_h1", align_bytes=64)
+        wo_q = [sb.tile([P, 256], I32, name="wo_q%d" % s, align_bytes=64) for s in range(2)]
+        ident_f = sb.tile([P, P], F32, name="ident_f")
+        ident_b = sb.tile([P, P], BF16, name="ident_b")
+        brows = sb.tile([P, 512], BF16, name="brows")
+        bias_bc = sb.tile([P, D + 3 * H], BF16, name="bias_bc")
+        warm = sb.tile([P, 1], F32, name="warm")
+        warm2 = sb.tile([P, 1], F32, name="warm2")
+        grouped = [sb.tile([P, 1024], BF16, name="grouped%d" % a, align_bytes=64) for a in range(2)]
+        hq = [sb.tile([P, 256], I32, name="hq%d" % a, align_bytes=64) for a in range(2)]
+        hs = [sb.tile([P, 256], U8, name="hs%d" % a, align_bytes=64) for a in range(2)]
+        xf = sb.tile([P, D], F32, name="xf")
+        c_red = sb.tile([P, H], F32, name="c_red")
+        xu = sb.tile([P, H], F32, name="xu")
+        xi = sb.tile([P, H], F32, name="xi")
+        c_t = sb.tile([P, H], F32, name="c_t")
+        tanh_c = sb.tile([P, H], F32, name="tanh_c")
+        xo = sb.tile([P, H], F32, name="xo")
+        h_t = sb.tile([P, H], F32, name="h_t")
+
+        uf = U_f_w_words.rearrange("g p n t -> g p (n t)")
+        ui = U_iou_w_words.rearrange("g p n t -> g p (n t)")
+        ui_p = U_iou_w_words.rearrange("g p n t -> p g (n t)")
+
+        nc.vector.memset(planes_f[:].bitcast(I32), 0)
+        nc.vector.memset(warm[:], 0.0)
+        nc.vector.memset(planes_iou[:].bitcast(I32), 0)
+        nc.gpsimd.memset(brows[:], 0.0)
+        make_identity(nc, ident_f[:])
+        make_identity(nc, ident_b[:])
+
+        nc.scalar.dma_start(out=brows[0:4, :], in_=U_f_b[0:D].rearrange("(r c) -> r c", c=512))
+        nc.scalar.dma_start(out=brows[4:10, :], in_=b_iou.rearrange("o (r c) -> (o r) c", c=512))
+        nc.scalar.activation(out=warm2[:], in_=warm[:], func=ACT.Sigmoid)
+
+        def load_scales(planes, scales, width, pool_queue):
+            for q in range(4):
+                dst = planes[32 * q : 32 * q + 16, :]
+                src = scales[0:G, 4 * q : 4 * q + 4, 0:width]
+                if pool_queue:
+                    nc.gpsimd.dma_start(out=dst.bitcast(F32), in_=src.bitcast(F32))
+                else:
+                    nc.sync.dma_start(out=dst.bitcast(I32), in_=src.bitcast(I32))
+
+        nc.sync.dma_start(out=h_sb[:], in_=h_mail.rearrange("n k h -> n (k h)"))
+        load_scales(planes_f, U_f_w_scales, D, SCALES_F == "pool")
+        if SCALES_IOU != "mid":
+            load_scales(planes_iou, U_iou_w_scales, 3 * H, SCALES_IOU == "pool")
+        for g in range(G):
+            nc.sync.dma_start(out=wf[g][:], in_=uf[g, :, 0 : 4 * D].bitcast(I32))
+        if SCALES_IOU == "mid":
+            load_scales(planes_iou, U_iou_w_scales, 3 * H, False)
+        nc.sync.dma_start(out=c_sb[:], in_=c_mail.rearrange("n k h -> n (k h)"))
+        for g in range(G):
+            nc.sync.dma_start(out=wu[g][:], in_=ui[g, :, 8 * H : 12 * H].bitcast(I32))
+        for g in range(G - 1):
+            nc.sync.dma_start(out=wi[g][:], in_=ui[g, :, 0 : 4 * H].bitcast(I32))
+        for s in range(2):
+            nc.sync.dma_start(out=wi3[s][:], in_=ui[G - 1, :, 2048 * s : 2048 * (s + 1)].bitcast(I32))
+        nc.sync.dma_start(out=wo_h0[:], in_=ui_p[:, 0:G, 4 * H : 4 * H + 2048].bitcast(I32))
+        nc.sync.dma_start(out=wo_h1[:], in_=ui_p[:, 0 : G - 1, 4 * H + 2048 : 8 * H].bitcast(I32))
+        for s in range(2):
+            lo = 4 * H + 2048 + 1024 * s
+            nc.sync.dma_start(out=wo_q[s][:], in_=ui[G - 1, :, lo : lo + 1024].bitcast(I32))
+
+        h_words = h_sb[:].bitcast(F32)
+        xt = [bank(a, [P, 2, 2, P], F32, "xt%d" % a) for a in range(2)]
+        for a in range(2):
+            for gg in range(2):
+                g = 2 * a + gg
+                for u in range(2):
+                    nc.tensor.transpose(xt[a][:, gg, u, :], h_words[:, 256 * g + u : 256 * (g + 1) : 2], ident_f[:])
+        for a in range(2):
+            dst = grouped[a][:].bitcast(F32).rearrange("p (g n u) -> p g n u", g=2, u=2)
+            src = xt[a][:].rearrange("p g u n -> p g n u")
+            if a == 0:
+                nc.vector.tensor_copy(out=dst, in_=src)
+            else:
+                nc.scalar.copy(out=dst, in_=src)
+        for a in range(2):
+            nc.vector.quantize_mx(out=hq[a][:].bitcast(FP8X4), scales=hs[a][:], in_=grouped[a][:])
+
+        for t in range(5):
+            bps = bank(2 + t, [P, 1024], BF16, "bps%d" % t)
+            for s in range(2):
+                j = 2 * t + s
+                nc.tensor.matmul(
+                    out=bps[:, 512 * s : 512 * (s + 1)],
+                    lhsT=ident_b[:, j : j + 1].to_broadcast([P, P]),
+                    rhs=brows[:],
+                    start=True,
+                    stop=True,
+                )
+            nc.scalar.copy(out=bias_bc[:, 1024 * t : 1024 * (t + 1)], in_=bps[:])
+
+        def mx(out, g, words, planes, col, n, start, stop):
+            a, gg = divmod(g, 2)
+            nc.tensor.matmul_mx(
+                out=out,
+                lhsT=hq[a][:, P * gg : P * (gg + 1)].bitcast(FP8X4),
+                lhsT_scale=hs[a][:, P * gg : P * (gg + 1)],
+                rhs=words.bitcast(FP8X4),
+                rhs_scale=planes[4 * g : P, col : col + n],
+                start=start,
+                stop=stop,
+            )
+
+        def add_bias(dst, acc, col, n):
+            nc.vector.tensor_tensor(out=dst, in0=acc, in1=bias_bc[:, col : col + n], op=ALU.add)
+
+        f_ps = [bank((7 + b) % 8, [P, 512], F32, "f_ps%d" % b) for b in range(4)]
+        for g in range(G):
+            for b in range(4):
+                mx(f_ps[b][:], g, wf[g][:, 512 * b : 512 * (b + 1)], planes_f, 512 * b, 512, g == 0, g == G - 1)
+        for b in range(4):
+            add_bias(xf[:, 512 * b : 512 * (b + 1)], f_ps[b][:], 512 * b, 512)
+        for k in range(2):
+            nc.scalar.activation(out=xf[:, H * k : H * (k + 1)], in_=xf[:, H * k : H * (k + 1)], func=ACT.Sigmoid)
+        nc.vector.tensor_tensor(out=xf[:], in0=xf[:], in1=c_sb[:], op=ALU.mult)
+        nc.vector.tensor_tensor(out=c_red[:], in0=xf[:, 0:H], in1=xf[:, H:D], op=ALU.add)
+
+        u_ps = [bank(3 + b, [P, 512], F32, "u_ps%d" % b) for b in range(2)]
+        for g in range(G):
+            for b in range(2):
+                mx(u_ps[b][:], g, wu[g][:, 512 * b : 512 * (b + 1)], planes_iou, 2 * H + 512 * b, 512, g == 0, g == G - 1)
+        for b in range(2):
+            add_bias(xu[:, 512 * b : 512 * (b + 1)], u_ps[b][:], D + 2 * H + 512 * b, 512)
+        nc.scalar.activation(out=xu[:], in_=xu[:], func=ACT.Tanh)
+
+        i_ps = [bank(5 + b, [P, 512], F32, "i_ps%d" % b) for b in range(2)]
+        for g in range(G - 1):
+            for b in range(2):
+                mx(i_ps[b][:], g, wi[g][:, 512 * b : 512 * (b + 1)], planes_iou, 512 * b, 512, g == 0, False)
+        for b in range(2):
+            mx(i_ps[b][:], G - 1, wi3[b][:], planes_iou, 512 * b, 512, False, True)
+        for b in range(2):
+            add_bias(xi[:, 512 * b : 512 * (b + 1)], i_ps[b][:], D + 512 * b, 512)
+            nc.scalar.activation(out=xi[:, 512 * b : 512 * (b + 1)], in_=xi[:, 512 * b : 512 * (b + 1)], func=ACT.Sigmoid)
+        for b in range(2):
+            cols = slice(512 * b, 512 * (b + 1))
+            nc.vector.tensor_tensor(out=xi[:, cols], in0=xi[:, cols], in1=xu[:, cols], op=ALU.mult)
+            nc.vector.tensor_tensor(out=c_t[:, cols], in0=xi[:, cols], in1=c_red[:, cols], op=ALU.add)
+            nc.scalar.activation(out=tanh_c[:, cols], in_=c_t[:, cols], func=ACT.Tanh)
+            nc.sync.dma_start(out=out_1[:, cols], in_=c_t[:, cols])
+
+        o_ps0 = bank(7, [P, 512], F32, "o_ps0")
+        for g in range(G):
+            mx(o_ps0[:], g, wo_h0[:, g, :], planes_iou, H, 512, g == 0, g == G - 1)
+        o_psq = [bank(s, [P, 256], F32, "o_psq%d" % s) for s in range(2)]
+        for g in range(G - 1):
+            for s in range(2):
+                mx(o_psq[s][:], g, wo_h1[:, g, 256 * s : 256 * (s + 1)], planes_iou, H + 512 + 256 * s, 256, g == 0, False)
+        for s in range(2):
+            mx(o_psq[s][:], G - 1, wo_q[s][:], planes_iou, H + 512 + 256 * s, 256, False, True)
+        pieces = [(0, 512, o_ps0), (512, 256, o_psq[0]), (768, 256, o_psq[1])]
+        for lo, n, acc in pieces:
+            add_bias(xo[:, lo : lo + n], acc[:], D + H + lo, n)
+            nc.scalar.activation(out=xo[:, lo : lo + n], in_=xo[:, lo : lo + n], func=ACT.Sigmoid)
+        for lo, n, acc in pieces:
+            nc.vector.tensor_tensor(out=h_t[:, lo : lo + n], in0=xo[:, lo : lo + n], in1=tanh_c[:, lo : lo + n], op=ALU.mult)
+            nc.sync.dma_start(out=out_0[:, lo : lo + n], in_=h_t[:, lo : lo + n])

@@ -18,7 +18,7 @@ G = 4
 FLOPS = 2 * P * D * (D + 3 * H)
 BYTES = 2 * (P * D * 2) + G * P * (D + 3 * H) * 4 + G * 16 * (D + 3 * H) + (D + 3 * H) * 2 + 2 * P * H * 4
 
-SCALES_IOU = "mid"
+SCALES_IOU = "pool"
 SCALES_F = "sync"
 
 

@@ -38,13 +38,12 @@ def tile_treelstmcell_w_kernel(
         c_sb = sb.tile([P, D], BF16, name="c_sb")
         planes_f = sb.tile([P, D], U8, name="planes_f", align_bytes=64)
         planes_iou = sb.tile([P, 3 * H], U8, name="planes_iou", align_bytes=64)
-        wf = [sb.tile([P, D], I32, name="wf%d" % g, align_bytes=64) for g in range(G)]
+        wf = [[sb.tile([P, H], I32, name="wf%d_%d" % (k, g), align_bytes=64) for g in range(G)] for k in range(2)]
         wu = [sb.tile([P, H], I32, name="wu%d" % g, align_bytes=64) for g in range(G)]
-        wi = [sb.tile([P, H], I32, name="wi%d" % g, align_bytes=64) for g in range(G - 1)]
-        wi3 = [sb.tile([P, 512], I32, name="wi3_%d" % s, align_bytes=64) for s in range(2)]
-        wo_h0 = sb.tile([P, G, 512], I32, name="wo_h0", align_bytes=64)
-        wo_h1 = sb.tile([P, G - 1, 512], I32, name="wo_h1", align_bytes=64)
-        wo_q = [sb.tile([P, 256], I32, name="wo_q%d" % s, align_bytes=64) for s in range(2)]
+        wi = [[sb.tile([P, 512], I32, name="wi%d_%d" % (s, g), align_bytes=64) for g in range(G)] for s in range(2)]
+        wo0 = [sb.tile([P, 512], I32, name="wo0_%d" % g, align_bytes=64) for g in range(G)]
+        woq_a = [sb.tile([P, G - 1, 256], I32, name="woq_a%d" % s, align_bytes=64) for s in range(2)]
+        woq_b = [sb.tile([P, 256], I32, name="woq_b%d" % s, align_bytes=64) for s in range(2)]
         ident_f = sb.tile([P, P], F32, name="ident_f")
         ident_b = sb.tile([P, P], BF16, name="ident_b")
         brows = sb.tile([P, 512], BF16, name="brows")
@@ -57,11 +56,13 @@ def tile_treelstmcell_w_kernel(
         xf = sb.tile([P, D], F32, name="xf")
         c_red = sb.tile([P, H], F32, name="c_red")
         xu = sb.tile([P, H], F32, name="xu")
-        xi = sb.tile([P, H], F32, name="xi")
-        c_t = sb.tile([P, H], F32, name="c_t")
-        tanh_c = sb.tile([P, H], F32, name="tanh_c")
-        xo = sb.tile([P, H], F32, name="xo")
-        h_t = sb.tile([P, H], F32, name="h_t")
+        xi = [sb.tile([P, 512], F32, name="xi%d" % b) for b in range(2)]
+        c_t = [sb.tile([P, 512], F32, name="c_t%d" % b) for b in range(2)]
+        tanh_c = [sb.tile([P, 512], F32, name="tanh_c%d" % b) for b in range(2)]
+        xo0 = sb.tile([P, 512], F32, name="xo0")
+        xoq = [sb.tile([P, 256], F32, name="xoq%d" % s) for s in range(2)]
+        h0 = sb.tile([P, 512], F32, name="h0")
+        hq_t = [sb.tile([P, 256], F32, name="hq_t%d" % s) for s in range(2)]
 
         uf = U_f_w_words.rearrange("g p n t -> g p (n t)")
         ui = U_iou_w_words.rearrange("g p n t -> g p (n t)")
@@ -91,22 +92,24 @@ def tile_treelstmcell_w_kernel(
         load_scales(planes_f, U_f_w_scales, D, SCALES_F == "pool")
         if SCALES_IOU != "mid":
             load_scales(planes_iou, U_iou_w_scales, 3 * H, SCALES_IOU == "pool")
-        for g in range(G):
-            nc.sync.dma_start(out=wf[g][:], in_=uf[g, :, 0 : 4 * D].bitcast(I32))
+        for k in range(2):
+            for g in range(G):
+                nc.sync.dma_start(out=wf[k][g][:], in_=uf[g, :, 4 * H * k : 4 * H * (k + 1)].bitcast(I32))
+            if k == 0:
+                nc.sync.dma_start(out=c_sb[:], in_=c_mail.rearrange("n k h -> n (k h)"))
         if SCALES_IOU == "mid":
             load_scales(planes_iou, U_iou_w_scales, 3 * H, False)
-        nc.sync.dma_start(out=c_sb[:], in_=c_mail.rearrange("n k h -> n (k h)"))
         for g in range(G):
             nc.sync.dma_start(out=wu[g][:], in_=ui[g, :, 8 * H : 12 * H].bitcast(I32))
-        for g in range(G - 1):
-            nc.sync.dma_start(out=wi[g][:], in_=ui[g, :, 0 : 4 * H].bitcast(I32))
         for s in range(2):
-            nc.sync.dma_start(out=wi3[s][:], in_=ui[G - 1, :, 2048 * s : 2048 * (s + 1)].bitcast(I32))
-        nc.sync.dma_start(out=wo_h0[:], in_=ui_p[:, 0:G, 4 * H : 4 * H + 2048].bitcast(I32))
-        nc.sync.dma_start(out=wo_h1[:], in_=ui_p[:, 0 : G - 1, 4 * H + 2048 : 8 * H].bitcast(I32))
+            for g in range(G):
+                nc.sync.dma_start(out=wi[s][g][:], in_=ui[g, :, 2048 * s : 2048 * (s + 1)].bitcast(I32))
+        for g in range(G):
+            nc.sync.dma_start(out=wo0[g][:], in_=ui[g, :, 4 * H : 4 * H + 2048].bitcast(I32))
         for s in range(2):
             lo = 4 * H + 2048 + 1024 * s
-            nc.sync.dma_start(out=wo_q[s][:], in_=ui[G - 1, :, lo : lo + 1024].bitcast(I32))
+            nc.sync.dma_start(out=woq_a[s][:], in_=ui_p[:, 0 : G - 1, lo : lo + 1024].bitcast(I32))
+            nc.sync.dma_start(out=woq_b[s][:], in_=ui[G - 1, :, lo : lo + 1024].bitcast(I32))
 
         h_words = h_sb[:].bitcast(F32)
         xt = [bank(a, [P, 2, 2, P], F32, "xt%d" % a) for a in range(2)]
@@ -154,14 +157,16 @@ def tile_treelstmcell_w_kernel(
             nc.vector.tensor_tensor(out=dst, in0=acc, in1=bias_bc[:, col : col + n], op=ALU.add)
 
         f_ps = [bank((7 + b) % 8, [P, 512], F32, "f_ps%d" % b) for b in range(4)]
-        for g in range(G):
-            for b in range(4):
-                mx(f_ps[b][:], g, wf[g][:, 512 * b : 512 * (b + 1)], planes_f, 512 * b, 512, g == 0, g == G - 1)
-        for b in range(4):
-            add_bias(xf[:, 512 * b : 512 * (b + 1)], f_ps[b][:], 512 * b, 512)
         for k in range(2):
-            nc.scalar.activation(out=xf[:, H * k : H * (k + 1)], in_=xf[:, H * k : H * (k + 1)], func=ACT.Sigmoid)
-        nc.vector.tensor_tensor(out=xf[:], in0=xf[:], in1=c_sb[:], op=ALU.mult)
+            child = slice(H * k, H * (k + 1))
+            for g in range(G):
+                for b in range(2):
+                    mx(f_ps[2 * k + b][:], g, wf[k][g][:, 512 * b : 512 * (b + 1)], planes_f, H * k + 512 * b, 512, g == 0, g == G - 1)
+            for b in range(2):
+                lo = H * k + 512 * b
+                add_bias(xf[:, lo : lo + 512], f_ps[2 * k + b][:], lo, 512)
+            nc.scalar.activation(out=xf[:, child], in_=xf[:, child], func=ACT.Sigmoid)
+            nc.vector.tensor_tensor(out=xf[:, child], in0=xf[:, child], in1=c_sb[:, child], op=ALU.mult)
         nc.vector.tensor_tensor(out=c_red[:], in0=xf[:, 0:H], in1=xf[:, H:D], op=ALU.add)
 
         u_ps = [bank(3 + b, [P, 512], F32, "u_ps%d" % b) for b in range(2)]
@@ -170,37 +175,56 @@ def tile_treelstmcell_w_kernel(
                 mx(u_ps[b][:], g, wu[g][:, 512 * b : 512 * (b + 1)], planes_iou, 2 * H + 512 * b, 512, g == 0, g == G - 1)
         for b in range(2):
             add_bias(xu[:, 512 * b : 512 * (b + 1)], u_ps[b][:], D + 2 * H + 512 * b, 512)
-        nc.scalar.activation(out=xu[:], in_=xu[:], func=ACT.Tanh)
+            nc.scalar.activation(out=xu[:, 512 * b : 512 * (b + 1)], in_=xu[:, 512 * b : 512 * (b + 1)], func=ACT.Tanh)
+
+        def act(dst, src, func):
+            nc.scalar.activation(out=dst, in_=src, func=func)
+
+        def vtt(dst, a, b, op):
+            nc.vector.tensor_tensor(out=dst, in0=a, in1=b, op=op)
 
         i_ps = [bank(5 + b, [P, 512], F32, "i_ps%d" % b) for b in range(2)]
-        for g in range(G - 1):
-            for b in range(2):
-                mx(i_ps[b][:], g, wi[g][:, 512 * b : 512 * (b + 1)], planes_iou, 512 * b, 512, g == 0, False)
-        for b in range(2):
-            mx(i_ps[b][:], G - 1, wi3[b][:], planes_iou, 512 * b, 512, False, True)
-        for b in range(2):
-            add_bias(xi[:, 512 * b : 512 * (b + 1)], i_ps[b][:], D + 512 * b, 512)
-            nc.scalar.activation(out=xi[:, 512 * b : 512 * (b + 1)], in_=xi[:, 512 * b : 512 * (b + 1)], func=ACT.Sigmoid)
-        for b in range(2):
-            cols = slice(512 * b, 512 * (b + 1))
-            nc.vector.tensor_tensor(out=xi[:, cols], in0=xi[:, cols], in1=xu[:, cols], op=ALU.mult)
-            nc.vector.tensor_tensor(out=c_t[:, cols], in0=xi[:, cols], in1=c_red[:, cols], op=ALU.add)
-            nc.scalar.activation(out=tanh_c[:, cols], in_=c_t[:, cols], func=ACT.Tanh)
-            nc.sync.dma_start(out=out_1[:, cols], in_=c_t[:, cols])
-
         o_ps0 = bank(7, [P, 512], F32, "o_ps0")
-        for g in range(G):
-            mx(o_ps0[:], g, wo_h0[:, g, :], planes_iou, H, 512, g == 0, g == G - 1)
         o_psq = [bank(s, [P, 256], F32, "o_psq%d" % s) for s in range(2)]
-        for g in range(G - 1):
-            for s in range(2):
-                mx(o_psq[s][:], g, wo_h1[:, g, 256 * s : 256 * (s + 1)], planes_iou, H + 512 + 256 * s, 256, g == 0, False)
+
+        def i_passes(b):
+            for g in range(G):
+                mx(i_ps[b][:], g, wi[b][g][:], planes_iou, 512 * b, 512, g == 0, g == G - 1)
+
+        def q_passes(s):
+            for g in range(G - 1):
+                mx(o_psq[s][:], g, woq_a[s][:, g, :], planes_iou, H + 512 + 256 * s, 256, g == 0, False)
+            mx(o_psq[s][:], G - 1, woq_b[s][:], planes_iou, H + 512 + 256 * s, 256, False, True)
+
+        def i_chain(b):
+            i_passes(b)
+            quarters = [slice(256 * e, 256 * (e + 1)) for e in range(2)]
+            for e, cols in enumerate(quarters):
+                add_bias(xi[b][:, cols], i_ps[b][:, cols], D + 512 * b + 256 * e, 256)
+                act(xi[b][:, cols], xi[b][:, cols], ACT.Sigmoid)
+            for e, cols in enumerate(quarters):
+                lo = 512 * b + 256 * e
+                vtt(xi[b][:, cols], xi[b][:, cols], xu[:, lo : lo + 256], ALU.mult)
+                vtt(c_t[b][:, cols], xi[b][:, cols], c_red[:, lo : lo + 256], ALU.add)
+                act(tanh_c[b][:, cols], c_t[b][:, cols], ACT.Tanh)
+            nc.sync.dma_start(out=out_1[:, 512 * b : 512 * (b + 1)], in_=c_t[b][:])
+
+        i_chain(0)
+        i_chain(1)
+        for g in range(G):
+            mx(o_ps0[:], g, wo0[g][:], planes_iou, H, 512, g == 0, g == G - 1)
+        for e in range(2):
+            cols = slice(256 * e, 256 * (e + 1))
+            add_bias(xo0[:, cols], o_ps0[:, cols], D + H + 256 * e, 256)
+            act(xo0[:, cols], xo0[:, cols], ACT.Sigmoid)
+        for e in range(2):
+            cols = slice(256 * e, 256 * (e + 1))
+            vtt(h0[:, cols], xo0[:, cols], tanh_c[0][:, cols], ALU.mult)
+        nc.sync.dma_start(out=out_0[:, 0:512], in_=h0[:])
         for s in range(2):
-            mx(o_psq[s][:], G - 1, wo_q[s][:], planes_iou, H + 512 + 256 * s, 256, False, True)
-        pieces = [(0, 512, o_ps0), (512, 256, o_psq[0]), (768, 256, o_psq[1])]
-        for lo, n, acc in pieces:
-            add_bias(xo[:, lo : lo + n], acc[:], D + H + lo, n)
-            nc.scalar.activation(out=xo[:, lo : lo + n], in_=xo[:, lo : lo + n], func=ACT.Sigmoid)
-        for lo, n, acc in pieces:
-            nc.vector.tensor_tensor(out=h_t[:, lo : lo + n], in0=xo[:, lo : lo + n], in1=tanh_c[:, lo : lo + n], op=ALU.mult)
-            nc.sync.dma_start(out=out_0[:, lo : lo + n], in_=h_t[:, lo : lo + n])
+            q_passes(s)
+            add_bias(xoq[s][:], o_psq[s][:], D + H + 512 + 256 * s, 256)
+            act(xoq[s][:], xoq[s][:], ACT.Sigmoid)
+        for s in range(2):
+            vtt(hq_t[s][:], xoq[s][:], tanh_c[1][:, 256 * s : 256 * (s + 1)], ALU.mult)
+            nc.sync.dma_start(out=out_0[:, 512 + 256 * s : 768 + 256 * s], in_=hq_t[s][:])

@@ -19,7 +19,7 @@ FLOPS = 2 * P * D * (D + 3 * H)
 BYTES = 2 * (P * D * 2) + G * P * (D + 3 * H) * 4 + G * 16 * (D + 3 * H) + (D + 3 * H) * 2 + 2 * P * H * 4
 
 SCALES_IOU = "pool"
-SCALES_F = "sync"
+SCALES_F = "pool"
 
 
 def tile_treelstmcell_w_kernel(
@@ -38,12 +38,13 @@ def tile_treelstmcell_w_kernel(
         c_sb = sb.tile([P, D], BF16, name="c_sb")
         planes_f = sb.tile([P, D], U8, name="planes_f", align_bytes=64)
         planes_iou = sb.tile([P, 3 * H], U8, name="planes_iou", align_bytes=64)
-        wf = [[sb.tile([P, H], I32, name="wf%d_%d" % (k, g), align_bytes=64) for g in range(G)] for k in range(2)]
+        wf = [sb.tile([P, D], I32, name="wf%d" % g, align_bytes=64) for g in range(G)]
         wu = [sb.tile([P, H], I32, name="wu%d" % g, align_bytes=64) for g in range(G)]
-        wi = [[sb.tile([P, 512], I32, name="wi%d_%d" % (s, g), align_bytes=64) for g in range(G)] for s in range(2)]
-        wo0 = [sb.tile([P, 512], I32, name="wo0_%d" % g, align_bytes=64) for g in range(G)]
-        woq_a = [sb.tile([P, G - 1, 256], I32, name="woq_a%d" % s, align_bytes=64) for s in range(2)]
-        woq_b = [sb.tile([P, 256], I32, name="woq_b%d" % s, align_bytes=64) for s in range(2)]
+        wi = [sb.tile([P, H], I32, name="wi%d" % g, align_bytes=64) for g in range(G - 1)]
+        wi3 = [sb.tile([P, 512], I32, name="wi3_%d" % s, align_bytes=64) for s in range(2)]
+        wo_h0 = sb.tile([P, G, 512], I32, name="wo_h0", align_bytes=64)
+        wo_h1 = sb.tile([P, G - 1, 512], I32, name="wo_h1", align_bytes=64)
+        wo_q = [sb.tile([P, 256], I32, name="wo_q%d" % s, align_bytes=64) for s in range(2)]
         ident_f = sb.tile([P, P], F32, name="ident_f")
         ident_b = sb.tile([P, P], BF16, name="ident_b")
         brows = sb.tile([P, 512], BF16, name="brows")
@@ -56,13 +57,11 @@ def tile_treelstmcell_w_kernel(
         xf = sb.tile([P, D], F32, name="xf")
         c_red = sb.tile([P, H], F32, name="c_red")
         xu = sb.tile([P, H], F32, name="xu")
-        xi = [sb.tile([P, 512], F32, name="xi%d" % b) for b in range(2)]
-        c_t = [sb.tile([P, 512], F32, name="c_t%d" % b) for b in range(2)]
-        tanh_c = [sb.tile([P, 512], F32, name="tanh_c%d" % b) for b in range(2)]
-        xo0 = sb.tile([P, 512], F32, name="xo0")
-        xoq = [sb.tile([P, 256], F32, name="xoq%d" % s) for s in range(2)]
-        h0 = sb.tile([P, 512], F32, name="h0")
-        hq_t = [sb.tile([P, 256], F32, name="hq_t%d" % s) for s in range(2)]
+        xi = sb.tile([P, H], F32, name="xi")
+        c_t = sb.tile([P, H], F32, name="c_t")
+        tanh_c = sb.tile([P, H], F32, name="tanh_c")
+        xo = sb.tile([P, H], F32, name="xo")
+        h_t = sb.tile([P, H], F32, name="h_t")
 
         uf = U_f_w_words.rearrange("g p n t -> g p (n t)")
         ui = U_iou_w_words.rearrange("g p n t -> g p (n t)")
@@ -71,9 +70,9 @@ def tile_treelstmcell_w_kernel(
         nc.vector.memset(planes_f[:].bitcast(I32), 0)
         nc.vector.memset(warm[:], 0.0)
         nc.vector.memset(planes_iou[:].bitcast(I32), 0)
-        nc.gpsimd.memset(brows[:], 0.0)
+        nc.vector.memset(brows[:].bitcast(I32), 0)
         make_identity(nc, ident_f[:])
-        make_identity(nc, ident_b[:])
+        nc.vector.tensor_copy(out=ident_b[:], in_=ident_f[:])
 
         nc.scalar.dma_start(out=brows[0:4, :], in_=U_f_b[0:D].rearrange("(r c) -> r c", c=512))
         nc.scalar.dma_start(out=brows[4:10, :], in_=b_iou.rearrange("o (r c) -> (o r) c", c=512))
@@ -92,24 +91,22 @@ def tile_treelstmcell_w_kernel(
         load_scales(planes_f, U_f_w_scales, D, SCALES_F == "pool")
         if SCALES_IOU != "mid":
             load_scales(planes_iou, U_iou_w_scales, 3 * H, SCALES_IOU == "pool")
-        for k in range(2):
-            for g in range(G):
-                nc.sync.dma_start(out=wf[k][g][:], in_=uf[g, :, 4 * H * k : 4 * H * (k + 1)].bitcast(I32))
-            if k == 0:
-                nc.sync.dma_start(out=c_sb[:], in_=c_mail.rearrange("n k h -> n (k h)"))
+        for g in range(G):
+            nc.sync.dma_start(out=wf[g][:], in_=uf[g, :, 0 : 4 * D].bitcast(I32))
         if SCALES_IOU == "mid":
             load_scales(planes_iou, U_iou_w_scales, 3 * H, False)
+        nc.sync.dma_start(out=c_sb[:], in_=c_mail.rearrange("n k h -> n (k h)"))
         for g in range(G):
             nc.sync.dma_start(out=wu[g][:], in_=ui[g, :, 8 * H : 12 * H].bitcast(I32))
+        for g in range(G - 1):
+            nc.sync.dma_start(out=wi[g][:], in_=ui[g, :, 0 : 4 * H].bitcast(I32))
         for s in range(2):
-            for g in range(G):
-                nc.sync.dma_start(out=wi[s][g][:], in_=ui[g, :, 2048 * s : 2048 * (s + 1)].bitcast(I32))
-        for g in range(G):
-            nc.sync.dma_start(out=wo0[g][:], in_=ui[g, :, 4 * H : 4 * H + 2048].bitcast(I32))
+            nc.sync.dma_start(out=wi3[s][:], in_=ui[G - 1, :, 2048 * s : 2048 * (s + 1)].bitcast(I32))
+        nc.sync.dma_start(out=wo_h0[:], in_=ui_p[:, 0:G, 4 * H : 4 * H + 2048].bitcast(I32))
+        nc.sync.dma_start(out=wo_h1[:], in_=ui_p[:, 0 : G - 1, 4 * H + 2048 : 8 * H].bitcast(I32))
         for s in range(2):
             lo = 4 * H + 2048 + 1024 * s
-            nc.sync.dma_start(out=woq_a[s][:], in_=ui_p[:, 0 : G - 1, lo : lo + 1024].bitcast(I32))
-            nc.sync.dma_start(out=woq_b[s][:], in_=ui[G - 1, :, lo : lo + 1024].bitcast(I32))
+            nc.sync.dma_start(out=wo_q[s][:], in_=ui[G - 1, :, lo : lo + 1024].bitcast(I32))
 
         h_words = h_sb[:].bitcast(F32)
         xt = [bank(a, [P, 2, 2, P], F32, "xt%d" % a) for a in range(2)]
@@ -157,16 +154,14 @@ def tile_treelstmcell_w_kernel(
             nc.vector.tensor_tensor(out=dst, in0=acc, in1=bias_bc[:, col : col + n], op=ALU.add)
 
         f_ps = [bank((7 + b) % 8, [P, 512], F32, "f_ps%d" % b) for b in range(4)]
+        for g in range(G):
+            for b in range(4):
+                mx(f_ps[b][:], g, wf[g][:, 512 * b : 512 * (b + 1)], planes_f, 512 * b, 512, g == 0, g == G - 1)
+        for b in range(4):
+            add_bias(xf[:, 512 * b : 512 * (b + 1)], f_ps[b][:], 512 * b, 512)
         for k in range(2):
-            child = slice(H * k, H * (k + 1))
-            for g in range(G):
-                for b in range(2):
-                    mx(f_ps[2 * k + b][:], g, wf[k][g][:, 512 * b : 512 * (b + 1)], planes_f, H * k + 512 * b, 512, g == 0, g == G - 1)
-            for b in range(2):
-                lo = H * k + 512 * b
-                add_bias(xf[:, lo : lo + 512], f_ps[2 * k + b][:], lo, 512)
-            nc.scalar.activation(out=xf[:, child], in_=xf[:, child], func=ACT.Sigmoid)
-            nc.vector.tensor_tensor(out=xf[:, child], in0=xf[:, child], in1=c_sb[:, child], op=ALU.mult)
+            nc.scalar.activation(out=xf[:, H * k : H * (k + 1)], in_=xf[:, H * k : H * (k + 1)], func=ACT.Sigmoid)
+        nc.vector.tensor_tensor(out=xf[:], in0=xf[:], in1=c_sb[:], op=ALU.mult)
         nc.vector.tensor_tensor(out=c_red[:], in0=xf[:, 0:H], in1=xf[:, H:D], op=ALU.add)
 
         u_ps = [bank(3 + b, [P, 512], F32, "u_ps%d" % b) for b in range(2)]
@@ -175,56 +170,37 @@ def tile_treelstmcell_w_kernel(
                 mx(u_ps[b][:], g, wu[g][:, 512 * b : 512 * (b + 1)], planes_iou, 2 * H + 512 * b, 512, g == 0, g == G - 1)
         for b in range(2):
             add_bias(xu[:, 512 * b : 512 * (b + 1)], u_ps[b][:], D + 2 * H + 512 * b, 512)
-            nc.scalar.activation(out=xu[:, 512 * b : 512 * (b + 1)], in_=xu[:, 512 * b : 512 * (b + 1)], func=ACT.Tanh)
-
-        def act(dst, src, func):
-            nc.scalar.activation(out=dst, in_=src, func=func)
-
-        def vtt(dst, a, b, op):
-            nc.vector.tensor_tensor(out=dst, in0=a, in1=b, op=op)
+        nc.scalar.activation(out=xu[:], in_=xu[:], func=ACT.Tanh)
 
         i_ps = [bank(5 + b, [P, 512], F32, "i_ps%d" % b) for b in range(2)]
+        for g in range(G - 1):
+            for b in range(2):
+                mx(i_ps[b][:], g, wi[g][:, 512 * b : 512 * (b + 1)], planes_iou, 512 * b, 512, g == 0, False)
+        for b in range(2):
+            mx(i_ps[b][:], G - 1, wi3[b][:], planes_iou, 512 * b, 512, False, True)
+        for b in range(2):
+            add_bias(xi[:, 512 * b : 512 * (b + 1)], i_ps[b][:], D + 512 * b, 512)
+            nc.scalar.activation(out=xi[:, 512 * b : 512 * (b + 1)], in_=xi[:, 512 * b : 512 * (b + 1)], func=ACT.Sigmoid)
+        for b in range(2):
+            cols = slice(512 * b, 512 * (b + 1))
+            nc.vector.tensor_tensor(out=xi[:, cols], in0=xi[:, cols], in1=xu[:, cols], op=ALU.mult)
+            nc.vector.tensor_tensor(out=c_t[:, cols], in0=xi[:, cols], in1=c_red[:, cols], op=ALU.add)
+            nc.scalar.activation(out=tanh_c[:, cols], in_=c_t[:, cols], func=ACT.Tanh)
+            nc.sync.dma_start(out=out_1[:, cols], in_=c_t[:, cols])
+
         o_ps0 = bank(7, [P, 512], F32, "o_ps0")
-        o_psq = [bank(s, [P, 256], F32, "o_psq%d" % s) for s in range(2)]
-
-        def i_passes(b):
-            for g in range(G):
-                mx(i_ps[b][:], g, wi[b][g][:], planes_iou, 512 * b, 512, g == 0, g == G - 1)
-
-        def q_passes(s):
-            for g in range(G - 1):
-                mx(o_psq[s][:], g, woq_a[s][:, g, :], planes_iou, H + 512 + 256 * s, 256, g == 0, False)
-            mx(o_psq[s][:], G - 1, woq_b[s][:], planes_iou, H + 512 + 256 * s, 256, False, True)
-
-        def i_chain(b):
-            i_passes(b)
-            quarters = [slice(256 * e, 256 * (e + 1)) for e in range(2)]
-            for e, cols in enumerate(quarters):
-                add_bias(xi[b][:, cols], i_ps[b][:, cols], D + 512 * b + 256 * e, 256)
-                act(xi[b][:, cols], xi[b][:, cols], ACT.Sigmoid)
-            for e, cols in enumerate(quarters):
-                lo = 512 * b + 256 * e
-                vtt(xi[b][:, cols], xi[b][:, cols], xu[:, lo : lo + 256], ALU.mult)
-                vtt(c_t[b][:, cols], xi[b][:, cols], c_red[:, lo : lo + 256], ALU.add)
-                act(tanh_c[b][:, cols], c_t[b][:, cols], ACT.Tanh)
-            nc.sync.dma_start(out=out_1[:, 512 * b : 512 * (b + 1)], in_=c_t[b][:])
-
-        i_chain(0)
-        i_chain(1)
         for g in range(G):
-            mx(o_ps0[:], g, wo0[g][:], planes_iou, H, 512, g == 0, g == G - 1)
-        for e in range(2):
-            cols = slice(256 * e, 256 * (e + 1))
-            add_bias(xo0[:, cols], o_ps0[:, cols], D + H + 256 * e, 256)
-            act(xo0[:, cols], xo0[:, cols], ACT.Sigmoid)
-        for e in range(2):
-            cols = slice(256 * e, 256 * (e + 1))
-            vtt(h0[:, cols], xo0[:, cols], tanh_c[0][:, cols], ALU.mult)
-        nc.sync.dma_start(out=out_0[:, 0:512], in_=h0[:])
+            mx(o_ps0[:], g, wo_h0[:, g, :], planes_iou, H, 512, g == 0, g == G - 1)
+        o_psq = [bank(s, [P, 256], F32, "o_psq%d" % s) for s in range(2)]
+        for g in range(G - 1):
+            for s in range(2):
+                mx(o_psq[s][:], g, wo_h1[:, g, 256 * s : 256 * (s + 1)], planes_iou, H + 512 + 256 * s, 256, g == 0, False)
         for s in range(2):
-            q_passes(s)
-            add_bias(xoq[s][:], o_psq[s][:], D + H + 512 + 256 * s, 256)
-            act(xoq[s][:], xoq[s][:], ACT.Sigmoid)
-        for s in range(2):
-            vtt(hq_t[s][:], xoq[s][:], tanh_c[1][:, 256 * s : 256 * (s + 1)], ALU.mult)
-            nc.sync.dma_start(out=out_0[:, 512 + 256 * s : 768 + 256 * s], in_=hq_t[s][:])
+            mx(o_psq[s][:], G - 1, wo_q[s][:], planes_iou, H + 512 + 256 * s, 256, False, True)
+        pieces = [(0, 512, o_ps0), (512, 256, o_psq[0]), (768, 256, o_psq[1])]
+        for lo, n, acc in pieces:
+            add_bias(xo[:, lo : lo + n], acc[:], D + H + lo, n)
+            nc.scalar.activation(out=xo[:, lo : lo + n], in_=xo[:, lo : lo + n], func=ACT.Sigmoid)
+        for lo, n, acc in pieces:
+            nc.vector.tensor_tensor(out=h_t[:, lo : lo + n], in0=xo[:, lo : lo + n], in1=tanh_c[:, lo : lo + n], op=ALU.mult)
+            nc.sync.dma_start(out=out_0[:, lo : lo + n], in_=h_t[:, lo : lo + n])

@@ -158,19 +158,23 @@ def tile_treelstmcell_w_kernel(
             for b in range(4):
                 mx(f_ps[b][:], g, wf[g][:, 512 * b : 512 * (b + 1)], planes_f, 512 * b, 512, g == 0, g == G - 1)
         for b in range(4):
-            add_bias(xf[:, 512 * b : 512 * (b + 1)], f_ps[b][:], 512 * b, 512)
-        for k in range(2):
-            nc.scalar.activation(out=xf[:, H * k : H * (k + 1)], in_=xf[:, H * k : H * (k + 1)], func=ACT.Sigmoid)
-        nc.vector.tensor_tensor(out=xf[:], in0=xf[:], in1=c_sb[:], op=ALU.mult)
-        nc.vector.tensor_tensor(out=c_red[:], in0=xf[:, 0:H], in1=xf[:, H:D], op=ALU.add)
+            cols = slice(512 * b, 512 * (b + 1))
+            add_bias(xf[:, cols], f_ps[b][:], 512 * b, 512)
+            nc.scalar.activation(out=xf[:, cols], in_=xf[:, cols], func=ACT.Sigmoid)
 
         u_ps = [bank(3 + b, [P, 512], F32, "u_ps%d" % b) for b in range(2)]
         for g in range(G):
             for b in range(2):
                 mx(u_ps[b][:], g, wu[g][:, 512 * b : 512 * (b + 1)], planes_iou, 2 * H + 512 * b, 512, g == 0, g == G - 1)
+
+        for k in range(2):
+            cols = slice(H * k, H * (k + 1))
+            nc.vector.tensor_tensor(out=xf[:, cols], in0=xf[:, cols], in1=c_sb[:, cols], op=ALU.mult)
         for b in range(2):
-            add_bias(xu[:, 512 * b : 512 * (b + 1)], u_ps[b][:], D + 2 * H + 512 * b, 512)
-        nc.scalar.activation(out=xu[:], in_=xu[:], func=ACT.Tanh)
+            cols = slice(512 * b, 512 * (b + 1))
+            add_bias(xu[:, cols], u_ps[b][:], D + 2 * H + 512 * b, 512)
+            nc.scalar.activation(out=xu[:, cols], in_=xu[:, cols], func=ACT.Tanh)
+        nc.vector.tensor_tensor(out=c_red[:], in0=xf[:, 0:H], in1=xf[:, H:D], op=ALU.add)
 
         i_ps = [bank(5 + b, [P, 512], F32, "i_ps%d" % b) for b in range(2)]
         for g in range(G - 1):

@@ -42,8 +42,8 @@ def tile_treelstmcell_w_kernel(
         wu = [sb.tile([P, H], I32, name="wu%d" % g, align_bytes=64) for g in range(G)]
         wi = [sb.tile([P, H], I32, name="wi%d" % g, align_bytes=64) for g in range(G - 1)]
         wi3 = [sb.tile([P, 512], I32, name="wi3_%d" % s, align_bytes=64) for s in range(2)]
-        wo_h0 = sb.tile([P, G, 512], I32, name="wo_h0", align_bytes=64)
-        wo_h1 = sb.tile([P, G - 1, 512], I32, name="wo_h1", align_bytes=64)
+        wo_h0 = [sb.tile([P, 512], I32, name="wo_h0_%d" % g, align_bytes=64) for g in range(G)]
+        wo_h1 = [sb.tile([P, 512], I32, name="wo_h1_%d" % g, align_bytes=64) for g in range(G - 1)]
         wo_q = [sb.tile([P, 256], I32, name="wo_q%d" % s, align_bytes=64) for s in range(2)]
         ident_f = sb.tile([P, P], F32, name="ident_f")
         ident_b = sb.tile([P, P], BF16, name="ident_b")
@@ -102,8 +102,10 @@ def tile_treelstmcell_w_kernel(
             nc.sync.dma_start(out=wi[g][:], in_=ui[g, :, 0 : 4 * H].bitcast(I32))
         for s in range(2):
             nc.sync.dma_start(out=wi3[s][:], in_=ui[G - 1, :, 2048 * s : 2048 * (s + 1)].bitcast(I32))
-        nc.sync.dma_start(out=wo_h0[:], in_=ui_p[:, 0:G, 4 * H : 4 * H + 2048].bitcast(I32))
-        nc.sync.dma_start(out=wo_h1[:], in_=ui_p[:, 0 : G - 1, 4 * H + 2048 : 8 * H].bitcast(I32))
+        for g in range(G):
+            nc.sync.dma_start(out=wo_h0[g][:], in_=ui[g, :, 4 * H : 4 * H + 2048].bitcast(I32))
+        for g in range(G - 1):
+            nc.sync.dma_start(out=wo_h1[g][:], in_=ui[g, :, 4 * H + 2048 : 8 * H].bitcast(I32))
         for s in range(2):
             lo = 4 * H + 2048 + 1024 * s
             nc.sync.dma_start(out=wo_q[s][:], in_=ui[G - 1, :, lo : lo + 1024].bitcast(I32))
@@ -188,17 +190,19 @@ def tile_treelstmcell_w_kernel(
         for b in range(2):
             cols = slice(512 * b, 512 * (b + 1))
             nc.vector.tensor_tensor(out=xi[:, cols], in0=xi[:, cols], in1=xu[:, cols], op=ALU.mult)
+        for b in range(2):
+            cols = slice(512 * b, 512 * (b + 1))
             nc.vector.tensor_tensor(out=c_t[:, cols], in0=xi[:, cols], in1=c_red[:, cols], op=ALU.add)
             nc.scalar.activation(out=tanh_c[:, cols], in_=c_t[:, cols], func=ACT.Tanh)
             nc.sync.dma_start(out=out_1[:, cols], in_=c_t[:, cols])
 
         o_ps0 = bank(7, [P, 512], F32, "o_ps0")
         for g in range(G):
-            mx(o_ps0[:], g, wo_h0[:, g, :], planes_iou, H, 512, g == 0, g == G - 1)
+            mx(o_ps0[:], g, wo_h0[g][:], planes_iou, H, 512, g == 0, g == G - 1)
         o_psq = [bank(s, [P, 256], F32, "o_psq%d" % s) for s in range(2)]
         for g in range(G - 1):
             for s in range(2):
-                mx(o_psq[s][:], g, wo_h1[:, g, 256 * s : 256 * (s + 1)], planes_iou, H + 512 + 256 * s, 256, g == 0, False)
+                mx(o_psq[s][:], g, wo_h1[g][:, 256 * s : 256 * (s + 1)], planes_iou, H + 512 + 256 * s, 256, g == 0, False)
         for s in range(2):
             mx(o_psq[s][:], G - 1, wo_q[s][:], planes_iou, H + 512 + 256 * s, 256, False, True)
         pieces = [(0, 512, o_ps0), (512, 256, o_psq[0]), (768, 256, o_psq[1])]

@@ -42,9 +42,8 @@ def tile_treelstmcell_w_kernel(
         wu = [sb.tile([P, H], I32, name="wu%d" % g, align_bytes=64) for g in range(G)]
         wi = [sb.tile([P, H], I32, name="wi%d" % g, align_bytes=64) for g in range(G - 1)]
         wi3 = [sb.tile([P, 512], I32, name="wi3_%d" % s, align_bytes=64) for s in range(2)]
-        wo_h0 = [sb.tile([P, 512], I32, name="wo_h0_%d" % g, align_bytes=64) for g in range(G)]
-        wo_h1 = [sb.tile([P, 512], I32, name="wo_h1_%d" % g, align_bytes=64) for g in range(G - 1)]
-        wo_q = [sb.tile([P, 256], I32, name="wo_q%d" % s, align_bytes=64) for s in range(2)]
+        O_LOADS = [(0, 0, 512), (1, 0, 512), (2, 0, 512), (3, 0, 512), (0, 512, 512), (1, 512, 512), (2, 512, 512), (3, 512, 256), (3, 768, 256)]
+        wo = [sb.tile([P, n], I32, name="wo%d" % j, align_bytes=64) for j, (g, lo, n) in enumerate(O_LOADS)]
         ident_f = sb.tile([P, P], F32, name="ident_f")
         ident_b = sb.tile([P, P], BF16, name="ident_b")
         brows = sb.tile([P, 512], BF16, name="brows")
@@ -102,13 +101,8 @@ def tile_treelstmcell_w_kernel(
             nc.sync.dma_start(out=wi[g][:], in_=ui[g, :, 0 : 4 * H].bitcast(I32))
         for s in range(2):
             nc.sync.dma_start(out=wi3[s][:], in_=ui[G - 1, :, 2048 * s : 2048 * (s + 1)].bitcast(I32))
-        for g in range(G):
-            nc.sync.dma_start(out=wo_h0[g][:], in_=ui[g, :, 4 * H : 4 * H + 2048].bitcast(I32))
-        for g in range(G - 1):
-            nc.sync.dma_start(out=wo_h1[g][:], in_=ui[g, :, 4 * H + 2048 : 8 * H].bitcast(I32))
-        for s in range(2):
-            lo = 4 * H + 2048 + 1024 * s
-            nc.sync.dma_start(out=wo_q[s][:], in_=ui[G - 1, :, lo : lo + 1024].bitcast(I32))
+        for j, (g, lo, n) in enumerate(O_LOADS):
+            nc.sync.dma_start(out=wo[j][:], in_=ui[g, :, 4 * (H + lo) : 4 * (H + lo + n)].bitcast(I32))
 
         h_words = h_sb[:].bitcast(F32)
         xt = [bank(a, [P, 2, 2, P], F32, "xt%d" % a) for a in range(2)]
@@ -184,31 +178,38 @@ def tile_treelstmcell_w_kernel(
                 mx(i_ps[b][:], g, wi[g][:, 512 * b : 512 * (b + 1)], planes_iou, 512 * b, 512, g == 0, False)
         for b in range(2):
             mx(i_ps[b][:], G - 1, wi3[b][:], planes_iou, 512 * b, 512, False, True)
-        for b in range(2):
-            add_bias(xi[:, 512 * b : 512 * (b + 1)], i_ps[b][:], D + 512 * b, 512)
-            nc.scalar.activation(out=xi[:, 512 * b : 512 * (b + 1)], in_=xi[:, 512 * b : 512 * (b + 1)], func=ACT.Sigmoid)
-        for b in range(2):
-            cols = slice(512 * b, 512 * (b + 1))
-            nc.vector.tensor_tensor(out=xi[:, cols], in0=xi[:, cols], in1=xu[:, cols], op=ALU.mult)
-        for b in range(2):
-            cols = slice(512 * b, 512 * (b + 1))
-            nc.vector.tensor_tensor(out=c_t[:, cols], in0=xi[:, cols], in1=c_red[:, cols], op=ALU.add)
-            nc.scalar.activation(out=tanh_c[:, cols], in_=c_t[:, cols], func=ACT.Tanh)
-            nc.sync.dma_start(out=out_1[:, cols], in_=c_t[:, cols])
+        pieces = [(0, 512, bank(7, [P, 512], F32, "o_ps0")), (512, 256, bank(0, [P, 256], F32, "o_ps1")), (768, 256, bank(1, [P, 256], F32, "o_ps2"))]
+        for j, (g, lo, n) in enumerate(O_LOADS):
+            for plo, pn, acc in pieces:
+                if lo <= plo and plo + pn <= lo + n:
+                    mx(acc[:], g, wo[j][:, plo - lo : plo - lo + pn], planes_iou, H + plo, pn, g == 0, g == G - 1)
 
-        o_ps0 = bank(7, [P, 512], F32, "o_ps0")
-        for g in range(G):
-            mx(o_ps0[:], g, wo_h0[g][:], planes_iou, H, 512, g == 0, g == G - 1)
-        o_psq = [bank(s, [P, 256], F32, "o_psq%d" % s) for s in range(2)]
-        for g in range(G - 1):
-            for s in range(2):
-                mx(o_psq[s][:], g, wo_h1[g][:, 256 * s : 256 * (s + 1)], planes_iou, H + 512 + 256 * s, 256, g == 0, False)
-        for s in range(2):
-            mx(o_psq[s][:], G - 1, wo_q[s][:], planes_iou, H + 512 + 256 * s, 256, False, True)
-        pieces = [(0, 512, o_ps0), (512, 256, o_psq[0]), (768, 256, o_psq[1])]
-        for lo, n, acc in pieces:
+        def half(b):
+            return slice(512 * b, 512 * (b + 1))
+
+        def o_gate(j):
+            lo, n, acc = pieces[j]
             add_bias(xo[:, lo : lo + n], acc[:], D + H + lo, n)
             nc.scalar.activation(out=xo[:, lo : lo + n], in_=xo[:, lo : lo + n], func=ACT.Sigmoid)
-        for lo, n, acc in pieces:
+
+        def h_piece(lo, n):
             nc.vector.tensor_tensor(out=h_t[:, lo : lo + n], in0=xo[:, lo : lo + n], in1=tanh_c[:, lo : lo + n], op=ALU.mult)
             nc.sync.dma_start(out=out_0[:, lo : lo + n], in_=h_t[:, lo : lo + n])
+
+        for b in range(2):
+            add_bias(xi[:, half(b)], i_ps[b][:], D + 512 * b, 512)
+            nc.scalar.activation(out=xi[:, half(b)], in_=xi[:, half(b)], func=ACT.Sigmoid)
+        for b in range(2):
+            nc.vector.tensor_tensor(out=xi[:, half(b)], in0=xi[:, half(b)], in1=xu[:, half(b)], op=ALU.mult)
+        for b in range(2):
+            nc.vector.tensor_tensor(out=c_t[:, half(b)], in0=xi[:, half(b)], in1=c_red[:, half(b)], op=ALU.add)
+            nc.scalar.activation(out=tanh_c[:, half(b)], in_=c_t[:, half(b)], func=ACT.Tanh)
+            nc.sync.dma_start(out=out_1[:, half(b)], in_=c_t[:, half(b)])
+            if b == 0:
+                o_gate(0)
+        for j in range(1, 3):
+            o_gate(j)
+        h_piece(0, 256)
+        h_piece(256, 256)
+        h_piece(512, 256)
+        h_piece(768, 256)

@@ -196,16 +196,20 @@ def tile_treelstmcell_w_kernel(
             nc.vector.tensor_tensor(out=h_t[:, lo : lo + n], in0=xo[:, lo : lo + n], in1=tanh_c[:, lo : lo + n], op=ALU.mult)
             nc.sync.dma_start(out=out_0[:, lo : lo + n], in_=h_t[:, lo : lo + n])
 
-        for b in range(2):
-            add_bias(xi[:, half(b)], i_ps[b][:], D + 512 * b, 512)
-            nc.scalar.activation(out=xi[:, half(b)], in_=xi[:, half(b)], func=ACT.Sigmoid)
-        for b in range(2):
-            nc.vector.tensor_tensor(out=xi[:, half(b)], in0=xi[:, half(b)], in1=xu[:, half(b)], op=ALU.mult)
-        for b in range(2):
-            nc.vector.tensor_tensor(out=c_t[:, half(b)], in0=xi[:, half(b)], in1=c_red[:, half(b)], op=ALU.add)
-            nc.scalar.activation(out=tanh_c[:, half(b)], in_=c_t[:, half(b)], func=ACT.Tanh)
-            nc.sync.dma_start(out=out_1[:, half(b)], in_=c_t[:, half(b)])
-            if b == 0:
+        def quarter(q):
+            return slice(256 * q, 256 * (q + 1))
+
+        for q in range(4):
+            add_bias(xi[:, quarter(q)], i_ps[q // 2][:, 256 * (q % 2) : 256 * (q % 2 + 1)], D + 256 * q, 256)
+            nc.scalar.activation(out=xi[:, quarter(q)], in_=xi[:, quarter(q)], func=ACT.Sigmoid)
+        for q in range(4):
+            nc.vector.tensor_tensor(out=xi[:, quarter(q)], in0=xi[:, quarter(q)], in1=xu[:, quarter(q)], op=ALU.mult)
+        for q in range(4):
+            nc.vector.tensor_tensor(out=c_t[:, quarter(q)], in0=xi[:, quarter(q)], in1=c_red[:, quarter(q)], op=ALU.add)
+            nc.scalar.activation(out=tanh_c[:, quarter(q)], in_=c_t[:, quarter(q)], func=ACT.Tanh)
+            if q % 2 == 1:
+                nc.sync.dma_start(out=out_1[:, half(q // 2)], in_=c_t[:, half(q // 2)])
+            if q == 1:
                 o_gate(0)
         for j in range(1, 3):
             o_gate(j)

from contextlib import ExitStack

import concourse.mybir as mybir
from concourse.masks import make_identity

F32 = mybir.dt.float32
BF16 = mybir.dt.bfloat16
I32 = mybir.dt.int32
U8 = mybir.dt.uint8
FP8X4 = mybir.dt.float8_e4m3fn_x4
ACT = mybir.ActivationFunctionType
ALU = mybir.AluOpType

P = 128
H = 1024
D = 2 * H
G = 4
FLOPS = 2 * P * D * (D + 3 * H)
BYTES = 2 * (P * D * 2) + G * P * (D + 3 * H) * 4 + G * 16 * (D + 3 * H) + (D + 3 * H) * 2 + 2 * P * H * 4

SCALES_IOU = "pool"
SCALES_F = "pool"


def tile_treelstmcell_w_kernel(
    tc, h_mail, c_mail, U_f_w_words, U_f_w_scales, U_f_b, U_iou_w_words, U_iou_w_scales, b_iou, out_0, out_1
):
    nc = tc.nc
    with ExitStack() as ctx:
        ctx.enter_context(tc.manual_schedule())
        sb = ctx.enter_context(tc.tile_pool(name="sb", bufs=1))
        ps = ctx.enter_context(tc.psum_pool(name="ps", bufs=1))

        def bank(b, shape, dtype, name):
            return ps.tile(shape, dtype, name=name, tag="bank%d" % b)

        h_sb = sb.tile([P, D], BF16, name="h_sb")
        c_sb = sb.tile([P, D], BF16, name="c_sb")
        planes_f = sb.tile([P, D], U8, name="planes_f", align_bytes=64)
        planes_iou = sb.tile([P, 3 * H], U8, name="planes_iou", align_bytes=64)
        wf = [sb.tile([P, D], I32, name="wf%d" % g, align_bytes=64) for g in range(G)]
        wu = [sb.tile([P, H], I32, name="wu%d" % g, align_bytes=64) for g in range(G)]
        wi = [sb.tile([P, H], I32, name="wi%d" % g, align_bytes=64) for g in range(G - 1)]
        wi3 = [sb.tile([P, 512], I32, name="wi3_%d" % s, align_bytes=64) for s in range(2)]
        O_LOADS = [(0, 0, 512), (1, 0, 512), (2, 0, 512), (3, 0, 512), (0, 512, 512), (1, 512, 512), (2, 512, 512), (3, 512, 256), (3, 768, 256)]
        wo = [sb.tile([P, n], I32, name="wo%d" % j, align_bytes=64) for j, (g, lo, n) in enumerate(O_LOADS)]
        ident_f = sb.tile([P, P], F32, name="ident_f")
        ident_b = sb.tile([P, P], BF16, name="ident_b")
        brows = sb.tile([P, 512], BF16, name="brows")
        bias_bc = sb.tile([P, D + 3 * H], BF16, name="bias_bc")
        warm = sb.tile([P, 1], F32, name="warm")
        warm2 = sb.tile([P, 1], F32, name="warm2")
        grouped = [sb.tile([P, 1024], BF16, name="grouped%d" % a, align_bytes=64) for a in range(2)]
        hq = [sb.tile([P, 256], I32, name="hq%d" % a, align_bytes=64) for a in range(2)]
        hs = [sb.tile([P, 256], U8, name="hs%d" % a, align_bytes=64) for a in range(2)]
        xf = sb.tile([P, D], F32, name="xf")
        c_red = sb.tile([P, H], F32, name="c_red")
        xu = sb.tile([P, H], F32, name="xu")
        xi = sb.tile([P, H], F32, name="xi")
        c_t = sb.tile([P, H], F32, name="c_t")
        tanh_c = sb.tile([P, H], F32, name="tanh_c")
        xo = sb.tile([P, H], F32, name="xo")
        h_t = sb.tile([P, H], F32, name="h_t")

        uf = U_f_w_words.rearrange("g p n t -> g p (n t)")
        ui = U_iou_w_words.rearrange("g p n t -> g p (n t)")
        ui_p = U_iou_w_words.rearrange("g p n t -> p g (n t)")

        nc.vector.memset(planes_f[:].bitcast(I32), 0)
        nc.vector.memset(warm[:], 0.0)
        nc.vector.memset(planes_iou[:].bitcast(I32), 0)
        nc.vector.memset(brows[:].bitcast(I32), 0)
        make_identity(nc, ident_f[:])
        nc.vector.tensor_copy(out=ident_b[:], in_=ident_f[:])

        nc.scalar.dma_start(out=brows[0:4, :], in_=U_f_b[0:D].rearrange("(r c) -> r c", c=512))
        nc.scalar.dma_start(out=brows[4:10, :], in_=b_iou.rearrange("o (r c) -> (o r) c", c=512))
        nc.scalar.activation(out=warm2[:], in_=warm[:], func=ACT.Sigmoid)

        def load_scales(planes, scales, width, pool_queue):
            for q in range(4):
                dst = planes[32 * q : 32 * q + 16, :]
                src = scales[0:G, 4 * q : 4 * q + 4, 0:width]
                if pool_queue:
                    nc.gpsimd.dma_start(out=dst.bitcast(F32), in_=src.bitcast(F32))
                else:
                    nc.sync.dma_start(out=dst.bitcast(I32), in_=src.bitcast(I32))

        nc.sync.dma_start(out=h_sb[:], in_=h_mail.rearrange("n k h -> n (k h)"))
        load_scales(planes_f, U_f_w_scales, D, SCALES_F == "pool")
        if SCALES_IOU != "mid":
            load_scales(planes_iou, U_iou_w_scales, 3 * H, SCALES_IOU == "pool")
        for g in range(G):
            nc.sync.dma_start(out=wf[g][:], in_=uf[g, :, 0 : 4 * D].bitcast(I32))
        if SCALES_IOU == "mid":
            load_scales(planes_iou, U_iou_w_scales, 3 * H, False)
        nc.sync.dma_start(out=c_sb[:], in_=c_mail.rearrange("n k h -> n (k h)"))
        for g in range(G):
            nc.sync.dma_start(out=wu[g][:], in_=ui[g, :, 8 * H : 12 * H].bitcast(I32))
        for g in range(G - 1):
            nc.sync.dma_start(out=wi[g][:], in_=ui[g, :, 0 : 4 * H].bitcast(I32))
        for s in range(2):
            nc.sync.dma_start(out=wi3[s][:], in_=ui[G - 1, :, 2048 * s : 2048 * (s + 1)].bitcast(I32))
        for j, (g, lo, n) in enumerate(O_LOADS):
            nc.sync.dma_start(out=wo[j][:], in_=ui[g, :, 4 * (H + lo) : 4 * (H + lo + n)].bitcast(I32))

        h_words = h_sb[:].bitcast(F32)
        xt = [bank(a, [P, 2, 2, P], F32, "xt%d" % a) for a in range(2)]
        for a in range(2):
            for gg in range(2):
                g = 2 * a + gg
                for u in range(2):
                    nc.tensor.transpose(xt[a][:, gg, u, :], h_words[:, 256 * g + u : 256 * (g + 1) : 2], ident_f[:])
        for a in range(2):
            dst = grouped[a][:].bitcast(F32).rearrange("p (g n u) -> p g n u", g=2, u=2)
            src = xt[a][:].rearrange("p g u n -> p g n u")
            if a == 0:
                nc.vector.tensor_copy(out=dst, in_=src)
            else:
                nc.scalar.copy(out=dst, in_=src)
        for a in range(2):
            nc.vector.quantize_mx(out=hq[a][:].bitcast(FP8X4), scales=hs[a][:], in_=grouped[a][:])

        for t in range(5):
            bps = bank(2 + t, [P, 1024], BF16, "bps%d" % t)
            for s in range(2):
                j = 2 * t + s
                nc.tensor.matmul(
                    out=bps[:, 512 * s : 512 * (s + 1)],
                    lhsT=ident_b[:, j : j + 1].to_broadcast([P, P]),
                    rhs=brows[:],
                    start=True,
                    stop=True,
                )
            nc.scalar.copy(out=bias_bc[:, 1024 * t : 1024 * (t + 1)], in_=bps[:])

        def mx(out, g, words, planes, col, n, start, stop):
            a, gg = divmod(g, 2)
            nc.tensor.matmul_mx(
                out=out,
                lhsT=hq[a][:, P * gg : P * (gg + 1)].bitcast(FP8X4),
                lhsT_scale=hs[a][:, P * gg : P * (gg + 1)],
                rhs=words.bitcast(FP8X4),
                rhs_scale=planes[4 * g : P, col : col + n],
                start=start,
                stop=stop,
            )

        def add_bias(dst, acc, col, n):
            nc.vector.tensor_tensor(out=dst, in0=acc, in1=bias_bc[:, col : col + n], op=ALU.add)

        f_ps = [bank((7 + b) % 8, [P, 512], F32, "f_ps%d" % b) for b in range(4)]
        for g in range(G):
            for b in range(4):
                mx(f_ps[b][:], g, wf[g][:, 512 * b : 512 * (b + 1)], planes_f, 512 * b, 512, g == 0, g == G - 1)
        for b in range(4):
            cols = slice(512 * b, 512 * (b + 1))
            add_bias(xf[:, cols], f_ps[b][:], 512 * b, 512)
            nc.scalar.activation(out=xf[:, cols], in_=xf[:, cols], func=ACT.Sigmoid)

        u_ps = [bank(3 + b, [P, 512], F32, "u_ps%d" % b) for b in range(2)]
        for g in range(G):
            for b in range(2):
                mx(u_ps[b][:], g, wu[g][:, 512 * b : 512 * (b + 1)], planes_iou, 2 * H + 512 * b, 512, g == 0, g == G - 1)

        for k in range(2):
            cols = slice(H * k, H * (k + 1))
            nc.vector.tensor_tensor(out=xf[:, cols], in0=xf[:, cols], in1=c_sb[:, cols], op=ALU.mult)
        for b in range(2):
            cols = slice(512 * b, 512 * (b + 1))
            add_bias(xu[:, cols], u_ps[b][:], D + 2 * H + 512 * b, 512)
            nc.scalar.activation(out=xu[:, cols], in_=xu[:, cols], func=ACT.Tanh)
        nc.vector.tensor_tensor(out=c_red[:], in0=xf[:, 0:H], in1=xf[:, H:D], op=ALU.add)

        i_ps = [bank(5 + b, [P, 512], F32, "i_ps%d" % b) for b in range(2)]
        for g in range(G - 1):
            for b in range(2):
                mx(i_ps[b][:], g, wi[g][:, 512 * b : 512 * (b + 1)], planes_iou, 512 * b, 512, g == 0, False)
        for b in range(2):
            mx(i_ps[b][:], G - 1, wi3[b][:], planes_iou, 512 * b, 512, False, True)
        pieces = [(0, 512, bank(7, [P, 512], F32, "o_ps0")), (512, 256, bank(0, [P, 256], F32, "o_ps1")), (768, 256, bank(1, [P, 256], F32, "o_ps2"))]
        for j, (g, lo, n) in enumerate(O_LOADS):
            for plo, pn, acc in pieces:
                if lo <= plo and plo + pn <= lo + n:
                    mx(acc[:], g, wo[j][:, plo - lo : plo - lo + pn], planes_iou, H + plo, pn, g == 0, g == G - 1)

        def half(b):
            return slice(512 * b, 512 * (b + 1))

        def o_gate(j):
            lo, n, acc = pieces[j]
            add_bias(xo[:, lo : lo + n], acc[:], D + H + lo, n)
            nc.scalar.activation(out=xo[:, lo : lo + n], in_=xo[:, lo : lo + n], func=ACT.Sigmoid)

        def h_piece(lo, n):
            nc.vector.tensor_tensor(out=h_t[:, lo : lo + n], in0=xo[:, lo : lo + n], in1=tanh_c[:, lo : lo + n], op=ALU.mult)
            nc.sync.dma_start(out=out_0[:, lo : lo + n], in_=h_t[:, lo : lo + n])

        def quarter(q):
            return slice(256 * q, 256 * (q + 1))

        for q in range(4):
            add_bias(xi[:, quarter(q)], i_ps[q // 2][:, 256 * (q % 2) : 256 * (q % 2 + 1)], D + 256 * q, 256)
            nc.scalar.activation(out=xi[:, quarter(q)], in_=xi[:, quarter(q)], func=ACT.Sigmoid)
        for q in range(4):
            nc.vector.tensor_tensor(out=xi[:, quarter(q)], in0=xi[:, quarter(q)], in1=xu[:, quarter(q)], op=ALU.mult)
        for q in range(4):
            nc.vector.tensor_tensor(out=c_t[:, quarter(q)], in0=xi[:, quarter(q)], in1=c_red[:, quarter(q)], op=ALU.add)
            nc.scalar.activation(out=tanh_c[:, quarter(q)], in_=c_t[:, quarter(q)], func=ACT.Tanh)
            if q % 2 == 1:
                nc.sync.dma_start(out=out_1[:, half(q // 2)], in_=c_t[:, half(q // 2)])
            if q == 1:
                o_gate(0)
        for j in range(1, 3):
            o_gate(j)
        h_piece(0, 256)
        h_piece(256, 256)
        h_piece(512, 256)
        h_piece(768, 256)
